import numpy as np
import ml_dtypes


def mxq(x, axis, fmt="e4m3"):
    dtype, down = {"e4m3": (ml_dtypes.float8_e4m3fn, 7), "e5m2": (ml_dtypes.float8_e5m2, 14)}[fmt]
    v = np.moveaxis(np.asarray(x, np.float32).astype(ml_dtypes.bfloat16).astype(np.float64), axis, -1)
    blocks = v.reshape(v.shape[:-1] + (-1, 32))
    amax = np.abs(blocks).max(-1, keepdims=True)
    byte = np.maximum(np.where(amax > 0, np.frexp(amax)[1] - 1 + 127, 0) - down, 1)
    scale = np.exp2(byte - 127.0)
    codes = (blocks / scale).astype(np.float32).astype(dtype).astype(np.float64)
    return np.moveaxis((codes * scale).reshape(v.shape), -1, axis)


WIDE = False


def mx_kscale(k):
    if not WIDE:
        return np.ones(k)
    levels = np.array([10, -10, 5, -5, 0])
    a = np.random.permutation(np.resize(levels, k // 512 * 4)).reshape(k // 512, 4)
    idx = np.arange(k)
    return np.exp2(a[idx // 512, idx % 128 // 32])


BF16 = ml_dtypes.bfloat16


def bf(x):
    return np.asarray(x, np.float32).astype(BF16)


def f64(x):
    return np.asarray(x).astype(np.float64)


B, G, M, S, H = 256, 10, 4, 512, 512
ALPHA = 1.1


def entmax(alpha, v):
    v = v - np.max(v, axis=-1, keepdims=True)
    e = np.exp(v)
    s = (np.sum(e ** alpha, axis=-1, keepdims=True) + 1e-5) ** (1.0 / alpha)
    return e / s


def layernorm(h, w, b):
    mu = np.mean(h, axis=-1, keepdims=True)
    var = np.mean((h - mu) ** 2, axis=-1, keepdims=True)
    return (h - mu) * (1.0 / np.sqrt(var + 1e-5)) * w + b


def sigmoid(v):
    return 1.0 / (1.0 + np.exp(-v))


def group_matmul(a, w):
    nb, ng, nm, ns = a.shape
    y = a.transpose(1, 0, 2, 3).reshape(ng, nb * nm, ns) @ w.transpose(0, 2, 1)
    return y.reshape(ng, nb, nm, w.shape[1]).transpose(1, 0, 2, 3)


def setup_inputs():
    k = mx_kscale(S)
    ws = 0.003 * S ** (1.0 / ALPHA - 0.5)
    return {"x": bf(np.random.standard_normal((B, G * S)) * np.tile(k, G)),
            "W_masks": bf(np.random.standard_normal((G, M, S))),
            "W1": bf((np.random.standard_normal((G, H, S)) + 0.3) * ws / k),
            "W2": bf((np.random.standard_normal((G, H, S)) + 0.3) * ws / k),
            "ln1_w": bf(1.0 + 0.2 * np.random.standard_normal((G, H))),
            "ln1_b": bf(0.2 * np.random.standard_normal((G, H))),
            "ln2_w": bf(1.0 + 0.2 * np.random.standard_normal((G, H))),
            "ln2_b": bf(0.2 * np.random.standard_normal((G, H)))}


def reference(x, W_masks, W1, W2, ln1_w, ln1_b, ln2_w, ln2_b):
    g, m, s = W_masks.shape
    b = x.shape[0]
    xg = f64(x).reshape(b, g, s)
    mask = entmax(ALPHA, f64(W_masks))
    weighted = xg[:, :, None, :] * mask[None]
    wq = mxq(weighted, 3, "e4m3")
    h1 = group_matmul(wq, mxq(f64(W1), 2, "e4m3"))
    h2 = group_matmul(wq, mxq(f64(W2), 2, "e4m3"))
    n1 = layernorm(h1, f64(ln1_w)[None, :, None, :], f64(ln1_b)[None, :, None, :])
    n2 = layernorm(h2, f64(ln2_w)[None, :, None, :], f64(ln2_b)[None, :, None, :])
    activated = np.maximum(sigmoid(n1) * n2, 0.0)
    group_out = np.sum(activated, axis=2)
    return group_out.reshape(b, g * group_out.shape[-1])

@@ -1,0 +1,320 @@
+from contextlib import ExitStack
+
+import concourse.mybir as mybir
+from concourse.masks import make_identity
+
+F32 = mybir.dt.float32
+BF16 = mybir.dt.bfloat16
+U32 = mybir.dt.uint32
+U8 = mybir.dt.uint8
+FP8X4 = mybir.dt.float8_e4m3fn_x4
+ALU = mybir.AluOpType
+ACT = mybir.ActivationFunctionType
+AX = mybir.AxisListType
+
+B, G, M, S, H = 256, 10, 4, 512, 512
+ALPHA = 1.1
+P = 128
+FLOPS = 2 * 2 * B * G * M * S * H
+
+ACC = True
+NSTEP = G * 2 * M
+NSS = G * 2
+
+
+def tile_dynamicfeaturegroupinglayer_kernel(tc, x, W_masks, W1, W2, ln1_w, ln1_b, ln2_w, ln2_b, out):
+    nc = tc.nc
+    with ExitStack() as ctx:
+        ctx.enter_context(tc.manual_schedule())
+        const = ctx.enter_context(tc.tile_pool(name="const", bufs=1))
+        wrawp = ctx.enter_context(tc.tile_pool(name="wrawp", bufs=3))
+        prepp = ctx.enter_context(tc.tile_pool(name="prepp", bufs=2))
+        wtp = ctx.enter_context(tc.tile_pool(name="wtp", bufs=3))
+        small = ctx.enter_context(tc.tile_pool(name="small", bufs=4))
+        zp = ctx.enter_context(tc.tile_pool(name="zp", bufs=2))
+        ap3 = ctx.enter_context(tc.tile_pool(name="ap3", bufs=3))
+        outp = ctx.enter_context(tc.tile_pool(name="outp", bufs=2))
+        ph = ctx.enter_context(tc.psum_pool(name="ph", bufs=4))
+        pz = ctx.enter_context(tc.psum_pool(name="pz", bufs=2))
+        pprep = ctx.enter_context(tc.psum_pool(name="pprep", bufs=1))
+        pfin = ctx.enter_context(tc.psum_pool(name="pfin", bufs=1))
+
+        wm = const.tile([P, S], BF16, name="wm")
+        nc.sync.dma_start(out=wm[0:40, :], in_=W_masks.rearrange("g m s -> (g m) s"))
+        lnraw = const.tile([P, 2, P], BF16, name="lnraw")
+        nc.vector.memset(lnraw[:], 0.0)
+        nc.sync.dma_start(out=lnraw[0:40, 0, :], in_=ln1_w.rearrange("g (t p) -> (g t) p", p=P))
+        nc.sync.dma_start(out=lnraw[40:80, 0, :], in_=ln1_b.rearrange("g (t p) -> (g t) p", p=P))
+        nc.sync.dma_start(out=lnraw[0:40, 1, :], in_=ln2_w.rearrange("g (t p) -> (g t) p", p=P))
+        nc.sync.dma_start(out=lnraw[40:80, 1, :], in_=ln2_b.rearrange("g (t p) -> (g t) p", p=P))
+        x_sb = const.tile([P, 2, G * S], BF16, name="x_sb")
+        for bh in range(2):
+            nc.sync.dma_start(out=x_sb[:, bh, 0:S], in_=x[bh * P:(bh + 1) * P, 0:S])
+
+        wraw = {}
+
+        def load_w(g):
+            t_ = wrawp.tile([P, 2, 4, S], BF16, name="wraw", tag="wraw")
+            nc.sync.dma_start(out=t_[:, 0], in_=W1[g].rearrange("(t p) s -> p t s", p=P))
+            nc.sync.dma_start(out=t_[:, 1], in_=W2[g].rearrange("(t p) s -> p t s", p=P))
+            wraw[g] = t_
+
+        load_w(0)
+        for bh in range(2):
+            nc.sync.dma_start(out=x_sb[:, bh, S:G * S], in_=x[bh * P:(bh + 1) * P, S:G * S])
+        load_w(1)
+
+        ident = const.tile([P, P], F32, name="ident")
+        make_identity(nc, ident[:])
+        cexp = const.tile([P, 2], F32, name="cexp")
+        nc.vector.memset(cexp[:], -0.5)
+        one = const.tile([P, 1], F32, name="one")
+        nc.vector.memset(one[:], 1.0)
+        cal = const.tile([P, 1], F32, name="cal")
+        nc.vector.tensor_scalar(out=cal[:], in0=one[:], scalar1=-1.0 / ALPHA, scalar2=None, op0=ALU.mult)
+        mask_sb = const.tile([P, S], F32, name="mask_sb")
+        nc.vector.memset(mask_sb[:], 0.0)
+
+        mx_ = const.tile([P, 1], F32, name="mx_")
+        nc.vector.reduce_max(out=mx_[0:40, :], in_=wm[0:40, :], axis=AX.X)
+        nmx = const.tile([P, 1], F32, name="nmx")
+        nc.vector.tensor_scalar(out=nmx[0:40, :], in0=mx_[0:40, :], scalar1=-1.0, scalar2=None, op0=ALU.mult)
+        nmxa = const.tile([P, 1], F32, name="nmxa")
+        nc.vector.tensor_scalar(out=nmxa[0:40, :], in0=mx_[0:40, :], scalar1=-ALPHA, scalar2=None, op0=ALU.mult)
+        e_sb = const.tile([P, S], F32, name="e_sb")
+        nc.scalar.activation(out=e_sb[0:40, :], in_=wm[0:40, :], func=ACT.Exp, bias=nmx[0:40, :], scale=1.0)
+        ea_sb = const.tile([P, S], F32, name="ea_sb")
+        sa = const.tile([P, 1], F32, name="sa")
+        nc.scalar.activation(out=ea_sb[0:40, :], in_=wm[0:40, :], func=ACT.Exp, bias=nmxa[0:40, :], scale=ALPHA,
+                             accum_out=sa[0:40, :])
+        sae = const.tile([P, 1], F32, name="sae")
+        nc.vector.tensor_scalar(out=sae[0:40, :], in0=sa[0:40, :], scalar1=1e-5, scalar2=None, op0=ALU.add)
+        msc = const.tile([P, 1], F32, name="msc")
+        nc.gpsimd.tensor_tensor(out=msc[0:40, :], in0=sae[0:40, :], in1=cal[0:40, :], op=ALU.pow)
+        nc.vector.tensor_scalar(out=mask_sb[0:40, :], in0=e_sb[0:40, :], scalar1=msc[0:40, :], scalar2=None,
+                                op0=ALU.mult)
+        gw, wc, ws, xc, xs, xbank, wt, fillb = {}, {}, {}, {}, {}, {}, {}, {}
+
+        def wfill_t(g, f):
+            w, jh = f // 2, f % 2
+            bank = pprep.tile([P, 2, 256], F32, name="wbank", tag="prep")
+            for u in range(2):
+                for jl in range(2):
+                    src = wraw[g][:, w, 2 * jh + jl, :].bitcast(F32)
+                    nc.tensor.transpose(bank[:, u, jl * P:(jl + 1) * P], src[:, P * u:P * (u + 1)], ident[:])
+            fillb[(g, f)] = bank
+
+        def wfill_copy(g, f):
+            w, jh = f // 2, f % 2
+            if jh == 0:
+                gw[(g, w)] = prepp.tile([P, 4 * H], BF16, name="gw", tag="gw", align_bytes=64)
+            dst = gw[(g, w)][:].bitcast(F32).rearrange("p (j u) -> p j u", u=2)
+            nc.vector.tensor_copy(out=dst[:, jh * 256:(jh + 1) * 256, :], in_=fillb[(g, f)][:].rearrange("p u j -> p j u"))
+
+        def quant_w(g, w):
+            if w == 0:
+                wc[g] = prepp.tile([P, 2, H], U32, name="wc", tag="wc", align_bytes=64)
+                ws[g] = prepp.tile([P, 2, H], U8, name="ws", tag="ws", align_bytes=64)
+            nc.vector.quantize_mx(out=wc[g][:, w, :].bitcast(FP8X4), scales=ws[g][:, w, :], in_=gw[(g, w)][:])
+
+        def x_t(g):
+            bank = pprep.tile([P, 2, 256], F32, name="xbank", tag="prep")
+            for u in range(2):
+                for bh in range(2):
+                    src = x_sb[:, bh, :].bitcast(F32)
+                    nc.tensor.transpose(bank[:, u, bh * P:(bh + 1) * P],
+                                        src[:, 256 * g + P * u:256 * g + P * (u + 1)], ident[:])
+            xbank[g] = bank
+
+        def weighted(g, m):
+            t_ = wtp.tile([P, 4 * B], BF16, name="wt", tag="wt", align_bytes=64)
+            in0 = xbank[g][:].rearrange("p u b -> p (u b)").bitcast(BF16).rearrange("p (u b e) -> p b u e", u=2, e=2)
+            in1 = maskT[:, g * M + m, :].rearrange("p (u e) -> p u e", u=2).unsqueeze(1).to_broadcast([P, B, 2, 2])
+            nc.vector.tensor_tensor(out=t_[:].rearrange("p (b u e) -> p b u e", u=2, e=2), in0=in0, in1=in1,
+                                    op=ALU.mult)
+            wt[(g, m)] = t_
+
+        def quant_x(g, m):
+            if m == 0:
+                xc[g] = prepp.tile([P, M, B], U32, name="xc", tag="xc", align_bytes=64)
+                xs[g] = prepp.tile([P, M, B], U8, name="xs", tag="xs", align_bytes=64)
+            nc.vector.quantize_mx(out=xc[g][:, m, :].bitcast(FP8X4), scales=xs[g][:, m, :], in_=wt[(g, m)][:])
+
+        hb, mvs, rsd, zt, zbank, sig, r2, prod, finb = {}, {}, {}, {}, {}, {}, {}, {}, {}
+
+        def mx(t):
+            g, bh, m = t // 8, (t % 8) // 4, t % 4
+            cols = slice(bh * P, (bh + 1) * P)
+            pair = []
+            for w in range(2):
+                bank = ph.tile([P, H], F32, name="h", tag="h")
+                nc.tensor.matmul_mx(out=bank[:], lhsT=xc[g][:, m, cols].bitcast(FP8X4), lhsT_scale=xs[g][:, m, cols],
+                                    rhs=wc[g][:, w, :].bitcast(FP8X4), rhs_scale=ws[g][:, w, :],
+                                    start=True, stop=True)
+                pair.append(bank)
+            hb[t] = pair
+
+        def bn(t):
+            st = small.tile([P, 2, 6], F32, name="st", tag="st")
+            mv = small.tile([P, 2, 2], F32, name="mv", tag="mv")
+            for w in range(2):
+                nc.vector.bn_stats(out=st[:, w, :], in_=hb[t][w][:])
+            for w in range(2):
+                nc.vector.bn_aggr(out=mv[:, w, :], in_=st[:, w, :])
+            ve = small.tile([P, 2], F32, name="ve", tag="ve")
+            nc.vector.tensor_scalar(out=ve[:], in0=mv[:, :, 1], scalar1=1e-5, scalar2=None, op0=ALU.add)
+            nm = small.tile([P, 2], F32, name="nm", tag="nm")
+            nc.vector.tensor_scalar(out=nm[:], in0=mv[:, :, 0], scalar1=-1.0, scalar2=None, op0=ALU.mult)
+            mvs[t] = (ve, nm)
+
+        def ch(t):
+            ve, nm = mvs[t]
+            rs = small.tile([P, 2], F32, name="rs", tag="rs")
+            nc.gpsimd.tensor_tensor(out=rs[:], in0=ve[:], in1=cexp[:], op=ALU.pow)
+            nb = small.tile([P, 2], F32, name="nb", tag="nb")
+            nc.gpsimd.tensor_tensor(out=nb[:], in0=nm[:], in1=rs[:], op=ALU.mult)
+            rsd[t] = (rs, nb)
+
+        def zz(t):
+            ss, m = t // 4, t % 4
+            if m == 0:
+                zt[ss] = zp.tile([P, 2, M, H], F32, name="z", tag="z")
+            rs, nb = rsd[t]
+            for w in range(2):
+                nc.scalar.activation(out=zt[ss][:, w, m, :], in_=hb[t][w][:], func=ACT.Identity,
+                                     bias=nb[:, w:w + 1], scale=rs[:, w:w + 1])
+
+        def tr(ss, k):
+            jt, w = k // 2, k % 2
+            bank = pz.tile([P, M, P], F32, name="zT", tag="zT")
+            for m in range(M):
+                nc.tensor.transpose(bank[:, m, :], zt[ss][:, w, m, jt * P:(jt + 1) * P], ident[:])
+            zbank[(ss, k)] = bank
+
+        def act(ss, k):
+            jt, w = k // 2, k % 2
+            c = (ss // 2) * 4 + jt
+            src = zbank[(ss, k)][:].rearrange("p m b -> p (m b)")
+            if w == 0:
+                t_ = ap3.tile([P, M * P], F32, name="sig", tag="sig")
+                nc.scalar.activation(out=t_[:], in_=src, func=ACT.Sigmoid, bias=lnT[:, 0, 40 + c:41 + c],
+                                     scale=lnT[:, 0, c:c + 1])
+                sig[(ss, jt)] = t_
+            else:
+                t_ = ap3.tile([P, M * P], F32, name="r2", tag="r2")
+                nc.scalar.activation(out=t_[:], in_=src, func=ACT.Relu, bias=lnT[:, 1, 40 + c:41 + c],
+                                     scale=lnT[:, 1, c:c + 1])
+                r2[(ss, jt)] = t_
+
+        def mul(ss, jt):
+            t_ = ap3.tile([P, M, P], F32, name="prod", tag="prod")
+            nc.gpsimd.tensor_tensor(out=t_[:].rearrange("p m b -> p (m b)"), in0=sig[(ss, jt)][:], in1=r2[(ss, jt)][:],
+                                    op=ALU.mult)
+            prod[(ss, jt)] = t_
+
+        def acc(ss, jt):
+            if jt == 0:
+                finb[ss] = pfin.tile([P, H], F32, name="fin", tag="fin")
+            dst = finb[ss][:, jt * P:(jt + 1) * P]
+            if ACC:
+                for m in range(M):
+                    nc.tensor.matmul(dst, lhsT=prod[(ss, jt)][:, m, :], rhs=ident[:], is_transpose=True,
+                                     start=(m == 0), stop=(m == M - 1))
+            else:
+                a_ = ap3.tile([P, 2, P], F32, name="a_", tag="a_")
+                nc.gpsimd.tensor_tensor(out=a_[:], in0=prod[(ss, jt)][:, 0:2, :], in1=prod[(ss, jt)][:, 2:4, :],
+                                        op=ALU.add)
+                o_ = ap3.tile([P, P], F32, name="o_", tag="o_")
+                nc.gpsimd.tensor_tensor(out=o_[:], in0=a_[:, 0, :], in1=a_[:, 1, :], op=ALU.add)
+                nc.tensor.transpose(dst, o_[:], ident[:])
+
+        def fin(ss):
+            g, bh = ss // 2, ss % 2
+            ot = outp.tile([P, H], F32, name="ot", tag="ot")
+            nc.scalar.copy(out=ot[:], in_=finb[ss][:])
+            nc.sync.dma_start(out=out[bh * P:(bh + 1) * P, g * H:(g + 1) * H], in_=ot[:])
+
+        for f in range(4):
+            wfill_t(0, f)
+            wfill_copy(0, f)
+        lnf = const.tile([P, 2, P], F32, name="lnf")
+        nc.vector.tensor_copy(out=lnf[:], in_=lnraw[:])
+        lps = pz.tile([P, 2, P], F32, name="lps", tag="zT")
+        for a in range(2):
+            nc.tensor.transpose(lps[:, a, :], lnf[:, a, :], ident[:])
+        lnT = const.tile([P, 2, P], F32, name="lnT")
+        nc.vector.tensor_copy(out=lnT[:], in_=lps[:])
+
+        mps = pz.tile([P, 4, P], F32, name="mps", tag="zT")
+        for u in range(2):
+            for e in range(2):
+                nc.tensor.transpose(mps[:, 2 * u + e, :], mask_sb[:, 256 * u + e:256 * (u + 1):2], ident[:])
+        maskT = const.tile([P, G * M, 4], F32, name="maskT")
+        nc.vector.tensor_copy(out=maskT[:], in_=mps[:, :, 0:G * M].rearrange("p t c -> p c t"))
+
+        x_t(0)
+        weighted(0, 0)
+        quant_w(0, 0)
+        weighted(0, 1)
+        quant_w(0, 1)
+        quant_x(0, 0)
+        weighted(0, 2)
+        quant_x(0, 1)
+        weighted(0, 3)
+        quant_x(0, 2)
+        mx(0)
+        mx(1)
+        bn(0)
+        ch(0)
+        quant_x(0, 3)
+
+        for t in range(NSTEP + 5):
+            ss, m = t // 4, t % 4
+            prev = ss - 1
+            g, i = t // 8, t % 8
+            gn = g + 1
+            if i == 0 and g + 2 < G:
+                load_w(g + 2)
+            if t + 1 < NSTEP:
+                bn(t + 1)
+            if 0 <= prev < NSS:
+                act(prev, 2 * m)
+            pss, pjt = (prev, m - 1) if m >= 1 else (prev - 1, 3)
+            if 0 <= pss < NSS:
+                mul(pss, pjt)
+            if t + 1 < NSTEP:
+                ch(t + 1)
+            if t < NSTEP:
+                zz(t)
+            nss, nk = (prev, 2 * m + 2) if m < 3 else (ss, 0)
+            if 0 <= nss < NSS:
+                tr(nss, nk)
+            if 0 <= pss < NSS:
+                acc(pss, pjt)
+            if t + 2 < NSTEP:
+                mx(t + 2)
+            if gn < G:
+                if i < 4:
+                    wfill_t(gn, i)
+                elif i == 4:
+                    x_t(gn)
+            if 0 <= prev < NSS:
+                act(prev, 2 * m + 1)
+            nss, nk = (prev, 2 * m + 3) if m < 3 else (ss, 1)
+            if 0 <= nss < NSS:
+                tr(nss, nk)
+            if 0 <= pss < NSS and pjt == 3:
+                fin(pss)
+            if gn < G:
+                if i < 4:
+                    wfill_copy(gn, i)
+                if i == 2:
+                    quant_w(gn, 0)
+                if i == 4:
+                    quant_w(gn, 1)
+                if i >= 4:
+                    weighted(gn, i - 4)
+                if i >= 5:
+                    quant_x(gn, i - 5)
+            if i == 0 and 1 <= g < G:
+                quant_x(g, 3)

@@ -20,6 +20,7 @@ FLOPS = 2 * 2 * B * G * M * S * H
 ACC = True
 NSTEP = G * 2 * M
 NSS = G * 2
+OFF = -1
 
 
 def tile_dynamicfeaturegroupinglayer_kernel(tc, x, W_masks, W1, W2, ln1_w, ln1_b, ln2_w, ln2_b, out):
@@ -34,7 +35,8 @@ def tile_dynamicfeaturegroupinglayer_kernel(tc, x, W_masks, W1, W2, ln1_w, ln1_b
         zp = ctx.enter_context(tc.tile_pool(name="zp", bufs=2))
         ap3 = ctx.enter_context(tc.tile_pool(name="ap3", bufs=3))
         outp = ctx.enter_context(tc.tile_pool(name="outp", bufs=2))
-        ph = ctx.enter_context(tc.psum_pool(name="ph", bufs=4))
+        pa = ctx.enter_context(tc.psum_pool(name="pa", bufs=2))
+        pb = ctx.enter_context(tc.psum_pool(name="pb", bufs=2))
         pz = ctx.enter_context(tc.psum_pool(name="pz", bufs=2))
         pprep = ctx.enter_context(tc.psum_pool(name="pprep", bufs=1))
         pfin = ctx.enter_context(tc.psum_pool(name="pfin", bufs=1))
@@ -104,12 +106,16 @@ def tile_dynamicfeaturegroupinglayer_kernel(tc, x, W_masks, W1, W2, ln1_w, ln1_b
                     nc.tensor.transpose(bank[:, u, jl * P:(jl + 1) * P], src[:, P * u:P * (u + 1)], ident[:])
             fillb[(g, f)] = bank
 
-        def wfill_copy(g, f):
+        def wfill_copy(g, f, on_scalar=False):
             w, jh = f // 2, f % 2
             if jh == 0:
                 gw[(g, w)] = prepp.tile([P, 4 * H], BF16, name="gw", tag="gw", align_bytes=64)
             dst = gw[(g, w)][:].bitcast(F32).rearrange("p (j u) -> p j u", u=2)
-            nc.vector.tensor_copy(out=dst[:, jh * 256:(jh + 1) * 256, :], in_=fillb[(g, f)][:].rearrange("p u j -> p j u"))
+            src = fillb[(g, f)][:].rearrange("p u j -> p j u")
+            if on_scalar:
+                nc.scalar.copy(out=dst[:, jh * 256:(jh + 1) * 256, :], in_=src)
+            else:
+                nc.vector.tensor_copy(out=dst[:, jh * 256:(jh + 1) * 256, :], in_=src)
 
         def quant_w(g, w):
             if w == 0:
@@ -117,18 +123,18 @@ def tile_dynamicfeaturegroupinglayer_kernel(tc, x, W_masks, W1, W2, ln1_w, ln1_b
                 ws[g] = prepp.tile([P, 2, H], U8, name="ws", tag="ws", align_bytes=64)
             nc.vector.quantize_mx(out=wc[g][:, w, :].bitcast(FP8X4), scales=ws[g][:, w, :], in_=gw[(g, w)][:])
 
-        def x_t(g):
+        def x_t(g, half):
             bank = pprep.tile([P, 2, 256], F32, name="xbank", tag="prep")
             for u in range(2):
                 for bh in range(2):
                     src = x_sb[:, bh, :].bitcast(F32)
                     nc.tensor.transpose(bank[:, u, bh * P:(bh + 1) * P],
                                         src[:, 256 * g + P * u:256 * g + P * (u + 1)], ident[:])
-            xbank[g] = bank
+            xbank[(g, half)] = bank
 
         def weighted(g, m):
             t_ = wtp.tile([P, 4 * B], BF16, name="wt", tag="wt", align_bytes=64)
-            in0 = xbank[g][:].rearrange("p u b -> p (u b)").bitcast(BF16).rearrange("p (u b e) -> p b u e", u=2, e=2)
+            in0 = xbank[(g, m // 2)][:].rearrange("p u b -> p (u b)").bitcast(BF16).rearrange("p (u b e) -> p b u e", u=2, e=2)
             in1 = maskT[:, g * M + m, :].rearrange("p (u e) -> p u e", u=2).unsqueeze(1).to_broadcast([P, B, 2, 2])
             nc.vector.tensor_tensor(out=t_[:].rearrange("p (b u e) -> p b u e", u=2, e=2), in0=in0, in1=in1,
                                     op=ALU.mult)
@@ -140,25 +146,31 @@ def tile_dynamicfeaturegroupinglayer_kernel(tc, x, W_masks, W1, W2, ln1_w, ln1_b
                 xs[g] = prepp.tile([P, M, B], U8, name="xs", tag="xs", align_bytes=64)
             nc.vector.quantize_mx(out=xc[g][:, m, :].bitcast(FP8X4), scales=xs[g][:, m, :], in_=wt[(g, m)][:])
 
-        hb, mvs, rsd, zt, zbank, sig, r2, prod, finb = {}, {}, {}, {}, {}, {}, {}, {}, {}
+        ha, hb, mvs, rsd, zt, zbank, sig, r2, prod, finb = {}, {}, {}, {}, {}, {}, {}, {}, {}, {}
 
-        def mx(t):
+        def mx(t, second):
             g, bh, m = t // 8, (t % 8) // 4, t % 4
             cols = slice(bh * P, (bh + 1) * P)
             pair = []
             for w in range(2):
-                bank = ph.tile([P, H], F32, name="h", tag="h")
+                if second:
+                    bank = pb.tile([P, H], F32, name="hb", tag="hb")
+                else:
+                    bank = pa.tile([P, H], F32, name="ha", tag="ha")
                 nc.tensor.matmul_mx(out=bank[:], lhsT=xc[g][:, m, cols].bitcast(FP8X4), lhsT_scale=xs[g][:, m, cols],
                                     rhs=wc[g][:, w, :].bitcast(FP8X4), rhs_scale=ws[g][:, w, :],
                                     start=True, stop=True)
                 pair.append(bank)
-            hb[t] = pair
+            if second:
+                hb[t] = pair
+            else:
+                ha[t] = pair
 
         def bn(t):
             st = small.tile([P, 2, 6], F32, name="st", tag="st")
             mv = small.tile([P, 2, 2], F32, name="mv", tag="mv")
             for w in range(2):
-                nc.vector.bn_stats(out=st[:, w, :], in_=hb[t][w][:])
+                nc.vector.bn_stats(out=st[:, w, :], in_=ha[t][w][:])
             for w in range(2):
                 nc.vector.bn_aggr(out=mv[:, w, :], in_=st[:, w, :])
             ve = small.tile([P, 2], F32, name="ve", tag="ve")
@@ -236,7 +248,7 @@ def tile_dynamicfeaturegroupinglayer_kernel(tc, x, W_masks, W1, W2, ln1_w, ln1_b
 
         for f in range(4):
             wfill_t(0, f)
-            wfill_copy(0, f)
+            wfill_copy(0, f, on_scalar=True)
         lnf = const.tile([P, 2, P], F32, name="lnf")
         nc.vector.tensor_copy(out=lnf[:], in_=lnraw[:])
         lps = pz.tile([P, 2, P], F32, name="lps", tag="zT")
@@ -252,69 +264,83 @@ def tile_dynamicfeaturegroupinglayer_kernel(tc, x, W_masks, W1, W2, ln1_w, ln1_b
         maskT = const.tile([P, G * M, 4], F32, name="maskT")
         nc.vector.tensor_copy(out=maskT[:], in_=mps[:, :, 0:G * M].rearrange("p t c -> p c t"))
 
-        x_t(0)
+
+        def prep_v(g, k):
+            if k in (0, 1, 4, 5):
+                weighted(g, k if k < 2 else k - 2)
+            elif k in (2, 6):
+                wfill_copy(g, k // 2 - 1)
+                quant_x(g, k // 2 - 1)
+                quant_x(g, k // 2)
+            elif k in (3, 7):
+                wfill_copy(g, k // 2)
+                quant_w(g, k // 4)
+
+        def prep_pe(g, k):
+            if k in (-1, 3):
+                x_t(g, (k + 1) // 4)
+            elif k in (1, 2):
+                wfill_t(g, k - 1)
+            elif k in (5, 6):
+                wfill_t(g, k - 3)
+
+        def prep(t, on_pe):
+            for gq in range(1, G):
+                k = t - (8 * (gq - 1) + OFF)
+                if -1 <= k <= 7:
+                    if on_pe:
+                        prep_pe(gq, k)
+                    else:
+                        prep_v(gq, k)
+
+        x_t(0, 0)
         weighted(0, 0)
         quant_w(0, 0)
         weighted(0, 1)
         quant_w(0, 1)
+        x_t(0, 1)
         quant_x(0, 0)
         weighted(0, 2)
         quant_x(0, 1)
         weighted(0, 3)
         quant_x(0, 2)
-        mx(0)
-        mx(1)
-        bn(0)
-        ch(0)
+        mx(0, False)
         quant_x(0, 3)
+        for t in range(OFF - 1, 0):
+            prep(t, False)
+            prep(t, True)
 
-        for t in range(NSTEP + 5):
-            ss, m = t // 4, t % 4
-            prev = ss - 1
-            g, i = t // 8, t % 8
-            gn = g + 1
-            if i == 0 and g + 2 < G:
-                load_w(g + 2)
-            if t + 1 < NSTEP:
-                bn(t + 1)
-            if 0 <= prev < NSS:
-                act(prev, 2 * m)
-            pss, pjt = (prev, m - 1) if m >= 1 else (prev - 1, 3)
-            if 0 <= pss < NSS:
-                mul(pss, pjt)
-            if t + 1 < NSTEP:
-                ch(t + 1)
+        for t in range(NSTEP + 7):
+            if t % 8 == 0 and t // 8 + 2 < G:
+                load_w(t // 8 + 2)
             if t < NSTEP:
-                zz(t)
-            nss, nk = (prev, 2 * m + 2) if m < 3 else (ss, 0)
-            if 0 <= nss < NSS:
-                tr(nss, nk)
-            if 0 <= pss < NSS:
-                acc(pss, pjt)
-            if t + 2 < NSTEP:
-                mx(t + 2)
-            if gn < G:
-                if i < 4:
-                    wfill_t(gn, i)
-                elif i == 4:
-                    x_t(gn)
-            if 0 <= prev < NSS:
-                act(prev, 2 * m + 1)
-            nss, nk = (prev, 2 * m + 3) if m < 3 else (ss, 1)
-            if 0 <= nss < NSS:
-                tr(nss, nk)
-            if 0 <= pss < NSS and pjt == 3:
-                fin(pss)
-            if gn < G:
-                if i < 4:
-                    wfill_copy(gn, i)
-                if i == 2:
-                    quant_w(gn, 0)
-                if i == 4:
-                    quant_w(gn, 1)
-                if i >= 4:
-                    weighted(gn, i - 4)
-                if i >= 5:
-                    quant_x(gn, i - 5)
-            if i == 0 and 1 <= g < G:
-                quant_x(g, 3)
+                bn(t)
+            prep(t, False)
+            if t + 1 < NSTEP:
+                mx(t + 1, False)
+            if t < NSTEP:
+                ch(t)
+            tb = t - 1
+            if 0 <= tb < NSTEP:
+                mx(tb, True)
+            ta = tb - 4
+            sa, ma = ta // 4, ta % 4
+            if 0 <= sa < NSS:
+                tr(sa, 2 * ma)
+                tr(sa, 2 * ma + 1)
+            tm = ta - 1
+            sm, mm = tm // 4, tm % 4
+            if 0 <= sm < NSS:
+                mul(sm, mm)
+            if 0 <= tb < NSTEP:
+                zz(tb)
+            if 0 <= sa < NSS:
+                act(sa, 2 * ma)
+                act(sa, 2 * ma + 1)
+            tc_ = tm - 1
+            sc, mc = tc_ // 4, tc_ % 4
+            if 0 <= sc < NSS:
+                acc(sc, mc)
+                if mc == 3:
+                    fin(sc)
+            prep(t, True)

@@ -30,7 +30,7 @@ def tile_dynamicfeaturegroupinglayer_kernel(tc, x, W_masks, W1, W2, ln1_w, ln1_b
         const = ctx.enter_context(tc.tile_pool(name="const", bufs=1))
         wrawp = ctx.enter_context(tc.tile_pool(name="wrawp", bufs=3))
         prepp = ctx.enter_context(tc.tile_pool(name="prepp", bufs=2))
-        wtp = ctx.enter_context(tc.tile_pool(name="wtp", bufs=3))
+        wtp = ctx.enter_context(tc.tile_pool(name="wtp", bufs=4))
         small = ctx.enter_context(tc.tile_pool(name="small", bufs=4))
         zp = ctx.enter_context(tc.tile_pool(name="zp", bufs=2))
         ap3 = ctx.enter_context(tc.tile_pool(name="ap3", bufs=3))
@@ -123,18 +123,18 @@ def tile_dynamicfeaturegroupinglayer_kernel(tc, x, W_masks, W1, W2, ln1_w, ln1_b
                 ws[g] = prepp.tile([P, 2, H], U8, name="ws", tag="ws", align_bytes=64)
             nc.vector.quantize_mx(out=wc[g][:, w, :].bitcast(FP8X4), scales=ws[g][:, w, :], in_=gw[(g, w)][:])
 
-        def x_t(g, half):
+        def x_t(g):
             bank = pprep.tile([P, 2, 256], F32, name="xbank", tag="prep")
             for u in range(2):
                 for bh in range(2):
                     src = x_sb[:, bh, :].bitcast(F32)
                     nc.tensor.transpose(bank[:, u, bh * P:(bh + 1) * P],
                                         src[:, 256 * g + P * u:256 * g + P * (u + 1)], ident[:])
-            xbank[(g, half)] = bank
+            xbank[g] = bank
 
         def weighted(g, m):
             t_ = wtp.tile([P, 4 * B], BF16, name="wt", tag="wt", align_bytes=64)
-            in0 = xbank[(g, m // 2)][:].rearrange("p u b -> p (u b)").bitcast(BF16).rearrange("p (u b e) -> p b u e", u=2, e=2)
+            in0 = xbank[g][:].rearrange("p u b -> p (u b)").bitcast(BF16).rearrange("p (u b e) -> p b u e", u=2, e=2)
             in1 = maskT[:, g * M + m, :].rearrange("p (u e) -> p u e", u=2).unsqueeze(1).to_broadcast([P, B, 2, 2])
             nc.vector.tensor_tensor(out=t_[:].rearrange("p (b u e) -> p b u e", u=2, e=2), in0=in0, in1=in1,
                                     op=ALU.mult)
@@ -146,6 +146,7 @@ def tile_dynamicfeaturegroupinglayer_kernel(tc, x, W_masks, W1, W2, ln1_w, ln1_b
                 xs[g] = prepp.tile([P, M, B], U8, name="xs", tag="xs", align_bytes=64)
             nc.vector.quantize_mx(out=xc[g][:, m, :].bitcast(FP8X4), scales=xs[g][:, m, :], in_=wt[(g, m)][:])
 
+        sts, mvt, rst = {}, {}, {}
         ha, hb, mvs, rsd, zt, zbank, sig, r2, prod, finb = {}, {}, {}, {}, {}, {}, {}, {}, {}, {}
 
         def mx(t, second):
@@ -168,24 +169,32 @@ def tile_dynamicfeaturegroupinglayer_kernel(tc, x, W_masks, W1, W2, ln1_w, ln1_b
 
         def bn(t):
             st = small.tile([P, 2, 6], F32, name="st", tag="st")
-            mv = small.tile([P, 2, 2], F32, name="mv", tag="mv")
             for w in range(2):
                 nc.vector.bn_stats(out=st[:, w, :], in_=ha[t][w][:])
+            sts[t] = st
+
+        def ag(t):
+            mv = small.tile([P, 2, 2], F32, name="mv", tag="mv")
             for w in range(2):
-                nc.vector.bn_aggr(out=mv[:, w, :], in_=st[:, w, :])
+                nc.vector.bn_aggr(out=mv[:, w, :], in_=sts[t][:, w, :])
+            mvt[t] = mv
+
+        def vn(t):
             ve = small.tile([P, 2], F32, name="ve", tag="ve")
-            nc.vector.tensor_scalar(out=ve[:], in0=mv[:, :, 1], scalar1=1e-5, scalar2=None, op0=ALU.add)
+            nc.vector.tensor_scalar(out=ve[:], in0=mvt[t][:, :, 1], scalar1=1e-5, scalar2=None, op0=ALU.add)
             nm = small.tile([P, 2], F32, name="nm", tag="nm")
-            nc.vector.tensor_scalar(out=nm[:], in0=mv[:, :, 0], scalar1=-1.0, scalar2=None, op0=ALU.mult)
+            nc.vector.tensor_scalar(out=nm[:], in0=mvt[t][:, :, 0], scalar1=-1.0, scalar2=None, op0=ALU.mult)
             mvs[t] = (ve, nm)
 
-        def ch(t):
-            ve, nm = mvs[t]
+        def ch_rs(t):
             rs = small.tile([P, 2], F32, name="rs", tag="rs")
-            nc.gpsimd.tensor_tensor(out=rs[:], in0=ve[:], in1=cexp[:], op=ALU.pow)
+            nc.gpsimd.tensor_tensor(out=rs[:], in0=mvs[t][0][:], in1=cexp[:], op=ALU.pow)
+            rst[t] = rs
+
+        def ch_nb(t):
             nb = small.tile([P, 2], F32, name="nb", tag="nb")
-            nc.gpsimd.tensor_tensor(out=nb[:], in0=nm[:], in1=rs[:], op=ALU.mult)
-            rsd[t] = (rs, nb)
+            nc.gpsimd.tensor_tensor(out=nb[:], in0=mvs[t][1][:], in1=rst[t][:], op=ALU.mult)
+            rsd[t] = (rst[t], nb)
 
         def zz(t):
             ss, m = t // 4, t % 4
@@ -265,40 +274,36 @@ def tile_dynamicfeaturegroupinglayer_kernel(tc, x, W_masks, W1, W2, ln1_w, ln1_b
         nc.vector.tensor_copy(out=maskT[:], in_=mps[:, :, 0:G * M].rearrange("p t c -> p c t"))
 
 
-        def prep_v(g, k):
-            if k in (0, 1, 4, 5):
-                weighted(g, k if k < 2 else k - 2)
-            elif k in (2, 6):
-                wfill_copy(g, k // 2 - 1)
-                quant_x(g, k // 2 - 1)
-                quant_x(g, k // 2)
-            elif k in (3, 7):
-                wfill_copy(g, k // 2)
-                quant_w(g, k // 4)
+        def prep_v1(g, k, t):
+            if 0 <= k < 4:
+                weighted(g, k)
+            elif 4 <= k < 8:
+                wfill_copy(g, k - 4, on_scalar=(t < 8))
 
-        def prep_pe(g, k):
-            if k in (-1, 3):
-                x_t(g, (k + 1) // 4)
-            elif k in (1, 2):
-                wfill_t(g, k - 1)
-            elif k in (5, 6):
+        def prep_v2(g, k, t):
+            if k in (4, 5):
+                quant_x(g, 2 * k - 8)
+                quant_x(g, 2 * k - 7)
+            elif k in (6, 7):
+                quant_w(g, k - 6)
+
+        def prep_pe(g, k, t):
+            if k == -1:
+                x_t(g)
+            elif 3 <= k < 7:
                 wfill_t(g, k - 3)
 
-        def prep(t, on_pe):
+        def prep(t, part):
             for gq in range(1, G):
                 k = t - (8 * (gq - 1) + OFF)
                 if -1 <= k <= 7:
-                    if on_pe:
-                        prep_pe(gq, k)
-                    else:
-                        prep_v(gq, k)
+                    part(gq, k, t)
 
-        x_t(0, 0)
+        x_t(0)
         weighted(0, 0)
         quant_w(0, 0)
         weighted(0, 1)
         quant_w(0, 1)
-        x_t(0, 1)
         quant_x(0, 0)
         weighted(0, 2)
         quant_x(0, 1)
@@ -307,20 +312,26 @@ def tile_dynamicfeaturegroupinglayer_kernel(tc, x, W_masks, W1, W2, ln1_w, ln1_b
         mx(0, False)
         quant_x(0, 3)
         for t in range(OFF - 1, 0):
-            prep(t, False)
-            prep(t, True)
+            prep(t, prep_v1)
+            prep(t, prep_v2)
+            prep(t, prep_pe)
 
-        for t in range(NSTEP + 7):
+        for t in range(NSTEP + 8):
             if t % 8 == 0 and t // 8 + 2 < G:
                 load_w(t // 8 + 2)
             if t < NSTEP:
                 bn(t)
-            prep(t, False)
+            prep(t, prep_v1)
+            if 0 <= t - 1 < NSTEP:
+                vn(t - 1)
+            if t < NSTEP:
+                ag(t)
+            prep(t, prep_v2)
             if t + 1 < NSTEP:
                 mx(t + 1, False)
-            if t < NSTEP:
-                ch(t)
-            tb = t - 1
+            if 0 <= t - 1 < NSTEP:
+                ch_rs(t - 1)
+            tb = t - 2
             if 0 <= tb < NSTEP:
                 mx(tb, True)
             ta = tb - 4
@@ -332,6 +343,8 @@ def tile_dynamicfeaturegroupinglayer_kernel(tc, x, W_masks, W1, W2, ln1_w, ln1_b
             sm, mm = tm // 4, tm % 4
             if 0 <= sm < NSS:
                 mul(sm, mm)
+            if 0 <= t - 1 < NSTEP:
+                ch_nb(t - 1)
             if 0 <= tb < NSTEP:
                 zz(tb)
             if 0 <= sa < NSS:
@@ -343,4 +356,4 @@ def tile_dynamicfeaturegroupinglayer_kernel(tc, x, W_masks, W1, W2, ln1_w, ln1_b
                 acc(sc, mc)
                 if mc == 3:
                     fin(sc)
-            prep(t, True)
+            prep(t, prep_pe)

@@ -14,13 +14,15 @@ AX = mybir.AxisListType
 
 B, G, M, S, H = 256, 10, 4, 512, 512
 ALPHA = 1.1
+EPS = 1e-5
 P = 128
 FLOPS = 2 * 2 * B * G * M * S * H
 
-ACC = True
 NSTEP = G * 2 * M
 NSS = G * 2
-OFF = -1
+GM = G * M
+V_TAKES_Z = 72
+V_TAKES_RELU = 80
 
 
 def tile_dynamicfeaturegroupinglayer_kernel(tc, x, W_masks, W1, W2, ln1_w, ln1_b, ln2_w, ln2_b, out):
@@ -42,13 +44,7 @@ def tile_dynamicfeaturegroupinglayer_kernel(tc, x, W_masks, W1, W2, ln1_w, ln1_b
         pfin = ctx.enter_context(tc.psum_pool(name="pfin", bufs=1))
 
         wm = const.tile([P, S], BF16, name="wm")
-        nc.sync.dma_start(out=wm[0:40, :], in_=W_masks.rearrange("g m s -> (g m) s"))
-        lnraw = const.tile([P, 2, P], BF16, name="lnraw")
-        nc.vector.memset(lnraw[:], 0.0)
-        nc.sync.dma_start(out=lnraw[0:40, 0, :], in_=ln1_w.rearrange("g (t p) -> (g t) p", p=P))
-        nc.sync.dma_start(out=lnraw[40:80, 0, :], in_=ln1_b.rearrange("g (t p) -> (g t) p", p=P))
-        nc.sync.dma_start(out=lnraw[0:40, 1, :], in_=ln2_w.rearrange("g (t p) -> (g t) p", p=P))
-        nc.sync.dma_start(out=lnraw[40:80, 1, :], in_=ln2_b.rearrange("g (t p) -> (g t) p", p=P))
+        nc.sync.dma_start(out=wm[0:GM, :], in_=W_masks.rearrange("g m s -> (g m) s"))
         x_sb = const.tile([P, 2, G * S], BF16, name="x_sb")
         for bh in range(2):
             nc.sync.dma_start(out=x_sb[:, bh, 0:S], in_=x[bh * P:(bh + 1) * P, 0:S])
@@ -62,51 +58,62 @@ def tile_dynamicfeaturegroupinglayer_kernel(tc, x, W_masks, W1, W2, ln1_w, ln1_b
             wraw[g] = t_
 
         load_w(0)
+        lnraw = const.tile([P, 2, P], BF16, name="lnraw")
+        nc.vector.memset(lnraw[:], 0.0)
+        nc.sync.dma_start(out=lnraw[0:GM, 0, :], in_=ln1_w.rearrange("g (t p) -> (g t) p", p=P))
+        nc.sync.dma_start(out=lnraw[GM:2 * GM, 0, :], in_=ln1_b.rearrange("g (t p) -> (g t) p", p=P))
+        nc.sync.dma_start(out=lnraw[0:GM, 1, :], in_=ln2_w.rearrange("g (t p) -> (g t) p", p=P))
+        nc.sync.dma_start(out=lnraw[GM:2 * GM, 1, :], in_=ln2_b.rearrange("g (t p) -> (g t) p", p=P))
         for bh in range(2):
             nc.sync.dma_start(out=x_sb[:, bh, S:G * S], in_=x[bh * P:(bh + 1) * P, S:G * S])
         load_w(1)
 
         ident = const.tile([P, P], F32, name="ident")
         make_identity(nc, ident[:])
-        cexp = const.tile([P, 2], F32, name="cexp")
-        nc.vector.memset(cexp[:], -0.5)
         one = const.tile([P, 1], F32, name="one")
         nc.vector.memset(one[:], 1.0)
+        warm = const.tile([P, 1], F32, name="warm")
+        nc.scalar.activation(out=warm[:], in_=one[:], func=ACT.Exp)
+        cexp = const.tile([P, 2], F32, name="cexp")
+        nc.vector.memset(cexp[:], -0.5)
         cal = const.tile([P, 1], F32, name="cal")
         nc.vector.tensor_scalar(out=cal[:], in0=one[:], scalar1=-1.0 / ALPHA, scalar2=None, op0=ALU.mult)
         mask_sb = const.tile([P, S], F32, name="mask_sb")
         nc.vector.memset(mask_sb[:], 0.0)
 
         mx_ = const.tile([P, 1], F32, name="mx_")
-        nc.vector.reduce_max(out=mx_[0:40, :], in_=wm[0:40, :], axis=AX.X)
+        nc.vector.reduce_max(out=mx_[0:GM, :], in_=wm[0:GM, :], axis=AX.X)
         nmx = const.tile([P, 1], F32, name="nmx")
-        nc.vector.tensor_scalar(out=nmx[0:40, :], in0=mx_[0:40, :], scalar1=-1.0, scalar2=None, op0=ALU.mult)
+        nc.vector.tensor_scalar(out=nmx[0:GM, :], in0=mx_[0:GM, :], scalar1=-1.0, scalar2=None, op0=ALU.mult)
         nmxa = const.tile([P, 1], F32, name="nmxa")
-        nc.vector.tensor_scalar(out=nmxa[0:40, :], in0=mx_[0:40, :], scalar1=-ALPHA, scalar2=None, op0=ALU.mult)
-        e_sb = const.tile([P, S], F32, name="e_sb")
-        nc.scalar.activation(out=e_sb[0:40, :], in_=wm[0:40, :], func=ACT.Exp, bias=nmx[0:40, :], scale=1.0)
+        nc.vector.tensor_scalar(out=nmxa[0:GM, :], in0=mx_[0:GM, :], scalar1=-ALPHA, scalar2=None, op0=ALU.mult)
         ea_sb = const.tile([P, S], F32, name="ea_sb")
         sa = const.tile([P, 1], F32, name="sa")
-        nc.scalar.activation(out=ea_sb[0:40, :], in_=wm[0:40, :], func=ACT.Exp, bias=nmxa[0:40, :], scale=ALPHA,
-                             accum_out=sa[0:40, :])
+        nc.scalar.activation(out=ea_sb[0:GM, :], in_=wm[0:GM, :], func=ACT.Exp, bias=nmxa[0:GM, :], scale=ALPHA,
+                             accum_out=sa[0:GM, :])
+        e_sb = const.tile([P, S], F32, name="e_sb")
+        nc.scalar.activation(out=e_sb[0:GM, :], in_=wm[0:GM, :], func=ACT.Exp, bias=nmx[0:GM, :], scale=1.0)
         sae = const.tile([P, 1], F32, name="sae")
-        nc.vector.tensor_scalar(out=sae[0:40, :], in0=sa[0:40, :], scalar1=1e-5, scalar2=None, op0=ALU.add)
+        nc.vector.tensor_scalar(out=sae[0:GM, :], in0=sa[0:GM, :], scalar1=EPS, scalar2=None, op0=ALU.add)
         msc = const.tile([P, 1], F32, name="msc")
-        nc.gpsimd.tensor_tensor(out=msc[0:40, :], in0=sae[0:40, :], in1=cal[0:40, :], op=ALU.pow)
-        nc.vector.tensor_scalar(out=mask_sb[0:40, :], in0=e_sb[0:40, :], scalar1=msc[0:40, :], scalar2=None,
+        nc.gpsimd.tensor_tensor(out=msc[0:GM, :], in0=sae[0:GM, :], in1=cal[0:GM, :], op=ALU.pow)
+        nc.vector.tensor_scalar(out=mask_sb[0:GM, :], in0=e_sb[0:GM, :], scalar1=msc[0:GM, :], scalar2=None,
                                 op0=ALU.mult)
+        lnf = const.tile([P, 2, P], F32, name="lnf")
+        nc.vector.tensor_copy(out=lnf[:], in_=lnraw[:])
+
         gw, wc, ws, xc, xs, xbank, wt, fillb = {}, {}, {}, {}, {}, {}, {}, {}
 
-        def wfill_t(g, f):
+        def wfill_t(g, f, pool, tag):
             w, jh = f // 2, f % 2
-            bank = pprep.tile([P, 2, 256], F32, name="wbank", tag="prep")
+            bank = pool.tile([P, 2, 256], F32, name="wbank", tag=tag)
             for u in range(2):
                 for jl in range(2):
                     src = wraw[g][:, w, 2 * jh + jl, :].bitcast(F32)
                     nc.tensor.transpose(bank[:, u, jl * P:(jl + 1) * P], src[:, P * u:P * (u + 1)], ident[:])
             fillb[(g, f)] = bank
 
-        def wfill_copy(g, f, on_scalar=False):
+        def wfill_copy(g, f, on_scalar):
             w, jh = f // 2, f % 2
             if jh == 0:
                 gw[(g, w)] = prepp.tile([P, 4 * H], BF16, name="gw", tag="gw", align_bytes=64)
@@ -146,8 +153,8 @@ def tile_dynamicfeaturegroupinglayer_kernel(tc, x, W_masks, W1, W2, ln1_w, ln1_b
                 xs[g] = prepp.tile([P, M, B], U8, name="xs", tag="xs", align_bytes=64)
             nc.vector.quantize_mx(out=xc[g][:, m, :].bitcast(FP8X4), scales=xs[g][:, m, :], in_=wt[(g, m)][:])
 
-        sts, mvt, rst = {}, {}, {}
-        ha, hb, mvs, rsd, zt, zbank, sig, r2, prod, finb = {}, {}, {}, {}, {}, {}, {}, {}, {}, {}
+        sts, mvt, vet, nmt, rst, nbt = {}, {}, {}, {}, {}, {}
+        ha, hb, zt, zbank, sig, r2, prod, finb = {}, {}, {}, {}, {}, {}, {}, {}
 
         def mx(t, second):
             g, bh, m = t // 8, (t % 8) // 4, t % 4
@@ -168,42 +175,42 @@ def tile_dynamicfeaturegroupinglayer_kernel(tc, x, W_masks, W1, W2, ln1_w, ln1_b
                 ha[t] = pair
 
         def bn(t):
-            st = small.tile([P, 2, 6], F32, name="st", tag="st")
+            sts[t] = small.tile([P, 2, 6], F32, name="st", tag="st")
             for w in range(2):
-                nc.vector.bn_stats(out=st[:, w, :], in_=ha[t][w][:])
-            sts[t] = st
+                nc.vector.bn_stats(out=sts[t][:, w, :], in_=ha[t][w][:])
 
         def ag(t):
-            mv = small.tile([P, 2, 2], F32, name="mv", tag="mv")
+            mvt[t] = small.tile([P, 2, 2], F32, name="mv", tag="mv")
             for w in range(2):
-                nc.vector.bn_aggr(out=mv[:, w, :], in_=sts[t][:, w, :])
-            mvt[t] = mv
+                nc.vector.bn_aggr(out=mvt[t][:, w, :], in_=sts[t][:, w, :])
 
         def vn(t):
-            ve = small.tile([P, 2], F32, name="ve", tag="ve")
-            nc.vector.tensor_scalar(out=ve[:], in0=mvt[t][:, :, 1], scalar1=1e-5, scalar2=None, op0=ALU.add)
-            nm = small.tile([P, 2], F32, name="nm", tag="nm")
-            nc.vector.tensor_scalar(out=nm[:], in0=mvt[t][:, :, 0], scalar1=-1.0, scalar2=None, op0=ALU.mult)
-            mvs[t] = (ve, nm)
+            vet[t] = small.tile([P, 2], F32, name="ve", tag="ve")
+            nc.vector.tensor_scalar(out=vet[t][:], in0=mvt[t][:, :, 1], scalar1=EPS, scalar2=None, op0=ALU.add)
+            nmt[t] = small.tile([P, 2], F32, name="nm", tag="nm")
+            nc.vector.tensor_scalar(out=nmt[t][:], in0=mvt[t][:, :, 0], scalar1=-1.0, scalar2=None, op0=ALU.mult)
 
         def ch_rs(t):
-            rs = small.tile([P, 2], F32, name="rs", tag="rs")
-            nc.gpsimd.tensor_tensor(out=rs[:], in0=mvs[t][0][:], in1=cexp[:], op=ALU.pow)
-            rst[t] = rs
+            rst[t] = small.tile([P, 2], F32, name="rs", tag="rs")
+            nc.gpsimd.tensor_tensor(out=rst[t][:], in0=vet[t][:], in1=cexp[:], op=ALU.pow)
 
         def ch_nb(t):
-            nb = small.tile([P, 2], F32, name="nb", tag="nb")
-            nc.gpsimd.tensor_tensor(out=nb[:], in0=mvs[t][1][:], in1=rst[t][:], op=ALU.mult)
-            rsd[t] = (rst[t], nb)
+            nbt[t] = small.tile([P, 2], F32, name="nb", tag="nb")
+            nc.gpsimd.tensor_tensor(out=nbt[t][:], in0=nmt[t][:], in1=rst[t][:], op=ALU.mult)
 
-        def zz(t):
+        def z_dst(t, w):
             ss, m = t // 4, t % 4
-            if m == 0:
+            if ss not in zt:
                 zt[ss] = zp.tile([P, 2, M, H], F32, name="z", tag="z")
-            rs, nb = rsd[t]
-            for w in range(2):
-                nc.scalar.activation(out=zt[ss][:, w, m, :], in_=hb[t][w][:], func=ACT.Identity,
-                                     bias=nb[:, w:w + 1], scale=rs[:, w:w + 1])
+            return zt[ss][:, w, m, :]
+
+        def z_scalar(t, w):
+            nc.scalar.activation(out=z_dst(t, w), in_=hb[t][w][:], func=ACT.Identity,
+                                 bias=nbt[t][:, w:w + 1], scale=rst[t][:, w:w + 1])
+
+        def z_vector(t, w):
+            nc.vector.tensor_scalar(out=z_dst(t, w), in0=hb[t][w][:], scalar1=mvt[t][:, w, 0:1],
+                                    scalar2=rst[t][:, w:w + 1], op0=ALU.subtract, op1=ALU.mult)
 
         def tr(ss, k):
             jt, w = k // 2, k % 2
@@ -212,42 +219,38 @@ def tile_dynamicfeaturegroupinglayer_kernel(tc, x, W_masks, W1, W2, ln1_w, ln1_b
                 nc.tensor.transpose(bank[:, m, :], zt[ss][:, w, m, jt * P:(jt + 1) * P], ident[:])
             zbank[(ss, k)] = bank
 
-        def act(ss, k):
-            jt, w = k // 2, k % 2
+        def act_sig(ss, jt):
             c = (ss // 2) * 4 + jt
-            src = zbank[(ss, k)][:].rearrange("p m b -> p (m b)")
-            if w == 0:
-                t_ = ap3.tile([P, M * P], F32, name="sig", tag="sig")
-                nc.scalar.activation(out=t_[:], in_=src, func=ACT.Sigmoid, bias=lnT[:, 0, 40 + c:41 + c],
-                                     scale=lnT[:, 0, c:c + 1])
-                sig[(ss, jt)] = t_
-            else:
-                t_ = ap3.tile([P, M * P], F32, name="r2", tag="r2")
-                nc.scalar.activation(out=t_[:], in_=src, func=ACT.Relu, bias=lnT[:, 1, 40 + c:41 + c],
-                                     scale=lnT[:, 1, c:c + 1])
-                r2[(ss, jt)] = t_
+            sig[(ss, jt)] = ap3.tile([P, M * P], F32, name="sig", tag="sig")
+            nc.scalar.activation(out=sig[(ss, jt)][:], in_=zbank[(ss, 2 * jt)][:].rearrange("p m b -> p (m b)"),
+                                 func=ACT.Sigmoid, bias=lnT[:, 0, GM + c:GM + c + 1], scale=lnT[:, 0, c:c + 1])
 
-        def mul(ss, jt):
-            t_ = ap3.tile([P, M, P], F32, name="prod", tag="prod")
-            nc.gpsimd.tensor_tensor(out=t_[:].rearrange("p m b -> p (m b)"), in0=sig[(ss, jt)][:], in1=r2[(ss, jt)][:],
-                                    op=ALU.mult)
-            prod[(ss, jt)] = t_
+        def act_relu(ss, jt, on_vector):
+            c = (ss // 2) * 4 + jt
+            r2[(ss, jt)] = ap3.tile([P, M * P], F32, name="r2", tag="r2")
+            src = zbank[(ss, 2 * jt + 1)][:].rearrange("p m b -> p (m b)")
+            if on_vector:
+                nc.vector.tensor_scalar(out=r2[(ss, jt)][:], in0=src, scalar1=lnT[:, 1, c:c + 1],
+                                        scalar2=lnT[:, 1, GM + c:GM + c + 1], op0=ALU.mult, op1=ALU.add)
+            else:
+                nc.scalar.activation(out=r2[(ss, jt)][:], in_=src, func=ACT.Relu,
+                                     bias=lnT[:, 1, GM + c:GM + c + 1], scale=lnT[:, 1, c:c + 1])
+
+        def mul(ss, jt, on_vector):
+            prod[(ss, jt)] = ap3.tile([P, M, P], F32, name="prod", tag="prod")
+            dst = prod[(ss, jt)][:].rearrange("p m b -> p (m b)")
+            if on_vector:
+                nc.vector.scalar_tensor_tensor(out=dst, in0=r2[(ss, jt)][:], scalar=0.0, in1=sig[(ss, jt)][:],
+                                               op0=ALU.max, op1=ALU.mult)
+            else:
+                nc.gpsimd.tensor_tensor(out=dst, in0=sig[(ss, jt)][:], in1=r2[(ss, jt)][:], op=ALU.mult)
 
         def acc(ss, jt):
             if jt == 0:
                 finb[ss] = pfin.tile([P, H], F32, name="fin", tag="fin")
-            dst = finb[ss][:, jt * P:(jt + 1) * P]
-            if ACC:
-                for m in range(M):
-                    nc.tensor.matmul(dst, lhsT=prod[(ss, jt)][:, m, :], rhs=ident[:], is_transpose=True,
-                                     start=(m == 0), stop=(m == M - 1))
-            else:
-                a_ = ap3.tile([P, 2, P], F32, name="a_", tag="a_")
-                nc.gpsimd.tensor_tensor(out=a_[:], in0=prod[(ss, jt)][:, 0:2, :], in1=prod[(ss, jt)][:, 2:4, :],
-                                        op=ALU.add)
-                o_ = ap3.tile([P, P], F32, name="o_", tag="o_")
-                nc.gpsimd.tensor_tensor(out=o_[:], in0=a_[:, 0, :], in1=a_[:, 1, :], op=ALU.add)
-                nc.tensor.transpose(dst, o_[:], ident[:])
+            for m in range(M):
+                nc.tensor.matmul(finb[ss][:, jt * P:(jt + 1) * P], lhsT=prod[(ss, jt)][:, m, :], rhs=ident[:],
+                                 is_transpose=True, start=(m == 0), stop=(m == M - 1))
 
         def fin(ss):
             g, bh = ss // 2, ss % 2
@@ -255,30 +258,43 @@ def tile_dynamicfeaturegroupinglayer_kernel(tc, x, W_masks, W1, W2, ln1_w, ln1_b
             nc.scalar.copy(out=ot[:], in_=finb[ss][:])
             nc.sync.dma_start(out=out[bh * P:(bh + 1) * P, g * H:(g + 1) * H], in_=ot[:])
 
+        x_t(0)
         for f in range(4):
-            wfill_t(0, f)
-            wfill_copy(0, f, on_scalar=True)
-        lnf = const.tile([P, 2, P], F32, name="lnf")
-        nc.vector.tensor_copy(out=lnf[:], in_=lnraw[:])
-        lps = pz.tile([P, 2, P], F32, name="lps", tag="zT")
-        for a in range(2):
-            nc.tensor.transpose(lps[:, a, :], lnf[:, a, :], ident[:])
-        lnT = const.tile([P, 2, P], F32, name="lnT")
-        nc.vector.tensor_copy(out=lnT[:], in_=lps[:])
-
+            if f < 2:
+                wfill_t(0, f, pa, "ha")
+            else:
+                wfill_t(0, f, pb, "hb")
+            wfill_copy(0, f, True)
         mps = pz.tile([P, 4, P], F32, name="mps", tag="zT")
         for u in range(2):
             for e in range(2):
                 nc.tensor.transpose(mps[:, 2 * u + e, :], mask_sb[:, 256 * u + e:256 * (u + 1):2], ident[:])
-        maskT = const.tile([P, G * M, 4], F32, name="maskT")
-        nc.vector.tensor_copy(out=maskT[:], in_=mps[:, :, 0:G * M].rearrange("p t c -> p c t"))
-
+        lps = pz.tile([P, 2, P], F32, name="lps", tag="zT")
+        for a in range(2):
+            nc.tensor.transpose(lps[:, a, :], lnf[:, a, :], ident[:])
+        quant_w(0, 0)
+        maskT = const.tile([P, GM, 4], F32, name="maskT")
+        nc.vector.tensor_copy(out=maskT[:], in_=mps[:, :, 0:GM].rearrange("p t c -> p c t"))
+        weighted(0, 0)
+        quant_w(0, 1)
+        quant_x(0, 0)
+        mx(0, False)
+        weighted(0, 1)
+        lnT = const.tile([P, 2, P], F32, name="lnT")
+        nc.vector.tensor_copy(out=lnT[:], in_=lps[:])
+        quant_x(0, 1)
+        weighted(0, 2)
+        weighted(0, 3)
+        quant_x(0, 2)
+        x_t(1)
+        quant_x(0, 3)
+        weighted(1, 0)
 
         def prep_v1(g, k, t):
             if 0 <= k < 4:
                 weighted(g, k)
             elif 4 <= k < 8:
-                wfill_copy(g, k - 4, on_scalar=(t < 8))
+                wfill_copy(g, k - 4, t < 8)
 
         def prep_v2(g, k, t):
             if k in (4, 5):
@@ -291,69 +307,52 @@ def tile_dynamicfeaturegroupinglayer_kernel(tc, x, W_masks, W1, W2, ln1_w, ln1_b
             if k == -1:
                 x_t(g)
             elif 3 <= k < 7:
-                wfill_t(g, k - 3)
+                wfill_t(g, k - 3, pprep, "prep")
 
         def prep(t, part):
             for gq in range(1, G):
-                k = t - (8 * (gq - 1) + OFF)
+                k = t - (8 * (gq - 1) - 1)
                 if -1 <= k <= 7:
                     part(gq, k, t)
 
-        x_t(0)
-        weighted(0, 0)
-        quant_w(0, 0)
-        weighted(0, 1)
-        quant_w(0, 1)
-        quant_x(0, 0)
-        weighted(0, 2)
-        quant_x(0, 1)
-        weighted(0, 3)
-        quant_x(0, 2)
-        mx(0, False)
-        quant_x(0, 3)
-        for t in range(OFF - 1, 0):
-            prep(t, prep_v1)
-            prep(t, prep_v2)
-            prep(t, prep_pe)
-
         for t in range(NSTEP + 8):
+            tb = t - 2
+            ta = tb - 4
+            tm = ta - 1
+            tf = tm - 1
             if t % 8 == 0 and t // 8 + 2 < G:
                 load_w(t // 8 + 2)
+            if 0 <= tb < NSTEP:
+                mx(tb, True)
             if t < NSTEP:
                 bn(t)
             prep(t, prep_v1)
             if 0 <= t - 1 < NSTEP:
                 vn(t - 1)
+                ch_rs(t - 1)
+            if 0 <= tb < NSTEP and t >= V_TAKES_Z:
+                z_vector(tb, 1)
             if t < NSTEP:
                 ag(t)
             prep(t, prep_v2)
             if t + 1 < NSTEP:
                 mx(t + 1, False)
-            if 0 <= t - 1 < NSTEP:
-                ch_rs(t - 1)
-            tb = t - 2
-            if 0 <= tb < NSTEP:
-                mx(tb, True)
-            ta = tb - 4
-            sa, ma = ta // 4, ta % 4
-            if 0 <= sa < NSS:
-                tr(sa, 2 * ma)
-                tr(sa, 2 * ma + 1)
-            tm = ta - 1
-            sm, mm = tm // 4, tm % 4
-            if 0 <= sm < NSS:
-                mul(sm, mm)
+            if 0 <= ta < NSTEP:
+                tr(ta // 4, 2 * (ta % 4))
+                tr(ta // 4, 2 * (ta % 4) + 1)
+            if 0 <= tm < NSTEP:
+                mul(tm // 4, tm % 4, t - 1 >= V_TAKES_RELU)
             if 0 <= t - 1 < NSTEP:
                 ch_nb(t - 1)
             if 0 <= tb < NSTEP:
-                zz(tb)
-            if 0 <= sa < NSS:
-                act(sa, 2 * ma)
-                act(sa, 2 * ma + 1)
-            tc_ = tm - 1
-            sc, mc = tc_ // 4, tc_ % 4
-            if 0 <= sc < NSS:
-                acc(sc, mc)
-                if mc == 3:
-                    fin(sc)
+                z_scalar(tb, 0)
+                if t < V_TAKES_Z:
+                    z_scalar(tb, 1)
+            if 0 <= ta < NSTEP:
+                act_sig(ta // 4, ta % 4)
+                act_relu(ta // 4, ta % 4, t >= V_TAKES_RELU)
+            if 0 <= tf < NSTEP:
+                acc(tf // 4, tf % 4)
+                if tf % 4 == 3:
+                    fin(tf // 4)
             prep(t, prep_pe)

@@ -33,10 +33,10 @@ def tile_dynamicfeaturegroupinglayer_kernel(tc, x, W_masks, W1, W2, ln1_w, ln1_b
         wrawp = ctx.enter_context(tc.tile_pool(name="wrawp", bufs=3))
         prepp = ctx.enter_context(tc.tile_pool(name="prepp", bufs=2))
         wtp = ctx.enter_context(tc.tile_pool(name="wtp", bufs=4))
-        small = ctx.enter_context(tc.tile_pool(name="small", bufs=4))
+        small = ctx.enter_context(tc.tile_pool(name="small", bufs=6))
         zp = ctx.enter_context(tc.tile_pool(name="zp", bufs=2))
-        ap3 = ctx.enter_context(tc.tile_pool(name="ap3", bufs=3))
-        outp = ctx.enter_context(tc.tile_pool(name="outp", bufs=2))
+        ap3 = ctx.enter_context(tc.tile_pool(name="ap3", bufs=4))
+        outp = ctx.enter_context(tc.tile_pool(name="outp", bufs=3))
         pa = ctx.enter_context(tc.psum_pool(name="pa", bufs=2))
         pb = ctx.enter_context(tc.psum_pool(name="pb", bufs=2))
         pz = ctx.enter_context(tc.psum_pool(name="pz", bufs=2))
@@ -153,7 +153,7 @@ def tile_dynamicfeaturegroupinglayer_kernel(tc, x, W_masks, W1, W2, ln1_w, ln1_b
                 xs[g] = prepp.tile([P, M, B], U8, name="xs", tag="xs", align_bytes=64)
             nc.vector.quantize_mx(out=xc[g][:, m, :].bitcast(FP8X4), scales=xs[g][:, m, :], in_=wt[(g, m)][:])
 
-        sts, mvt, vet, nmt, rst, nbt = {}, {}, {}, {}, {}, {}
+        sts, mvt, vet, rst, nbt = {}, {}, {}, {}, {}
         ha, hb, zt, zbank, sig, r2, prod, finb = {}, {}, {}, {}, {}, {}, {}, {}
 
         def mx(t, second):
@@ -187,8 +187,6 @@ def tile_dynamicfeaturegroupinglayer_kernel(tc, x, W_masks, W1, W2, ln1_w, ln1_b
         def vn(t):
             vet[t] = small.tile([P, 2], F32, name="ve", tag="ve")
             nc.vector.tensor_scalar(out=vet[t][:], in0=mvt[t][:, :, 1], scalar1=EPS, scalar2=None, op0=ALU.add)
-            nmt[t] = small.tile([P, 2], F32, name="nm", tag="nm")
-            nc.vector.tensor_scalar(out=nmt[t][:], in0=mvt[t][:, :, 0], scalar1=-1.0, scalar2=None, op0=ALU.mult)
 
         def ch_rs(t):
             rst[t] = small.tile([P, 2], F32, name="rs", tag="rs")
@@ -196,7 +194,8 @@ def tile_dynamicfeaturegroupinglayer_kernel(tc, x, W_masks, W1, W2, ln1_w, ln1_b
 
         def ch_nb(t):
             nbt[t] = small.tile([P, 2], F32, name="nb", tag="nb")
-            nc.gpsimd.tensor_tensor(out=nbt[t][:], in0=nmt[t][:], in1=rst[t][:], op=ALU.mult)
+            nc.vector.scalar_tensor_tensor(out=nbt[t][:], in0=mvt[t][:, :, 0], scalar=-1.0, in1=rst[t][:],
+                                           op0=ALU.mult, op1=ALU.mult)
 
         def z_dst(t, w):
             ss, m = t // 4, t % 4
@@ -265,6 +264,7 @@ def tile_dynamicfeaturegroupinglayer_kernel(tc, x, W_masks, W1, W2, ln1_w, ln1_b
             else:
                 wfill_t(0, f, pb, "hb")
             wfill_copy(0, f, True)
+        nc.scalar.activation(out=warm[:], in_=one[:], func=ACT.Sigmoid)
         mps = pz.tile([P, 4, P], F32, name="mps", tag="zT")
         for u in range(2):
             for e in range(2):
@@ -326,6 +326,8 @@ def tile_dynamicfeaturegroupinglayer_kernel(tc, x, W_masks, W1, W2, ln1_w, ln1_b
                 mx(tb, True)
             if t < NSTEP:
                 bn(t)
+            if 0 <= tb < NSTEP:
+                ch_nb(tb)
             prep(t, prep_v1)
             if 0 <= t - 1 < NSTEP:
                 vn(t - 1)
@@ -342,8 +344,6 @@ def tile_dynamicfeaturegroupinglayer_kernel(tc, x, W_masks, W1, W2, ln1_w, ln1_b
                 tr(ta // 4, 2 * (ta % 4) + 1)
             if 0 <= tm < NSTEP:
                 mul(tm // 4, tm % 4, t - 1 >= V_TAKES_RELU)
-            if 0 <= t - 1 < NSTEP:
-                ch_nb(t - 1)
             if 0 <= tb < NSTEP:
                 z_scalar(tb, 0)
                 if t < V_TAKES_Z:

@@ -33,10 +33,10 @@ def tile_dynamicfeaturegroupinglayer_kernel(tc, x, W_masks, W1, W2, ln1_w, ln1_b
         wrawp = ctx.enter_context(tc.tile_pool(name="wrawp", bufs=3))
         prepp = ctx.enter_context(tc.tile_pool(name="prepp", bufs=2))
         wtp = ctx.enter_context(tc.tile_pool(name="wtp", bufs=4))
-        small = ctx.enter_context(tc.tile_pool(name="small", bufs=6))
+        small = ctx.enter_context(tc.tile_pool(name="small", bufs=4))
         zp = ctx.enter_context(tc.tile_pool(name="zp", bufs=2))
-        ap3 = ctx.enter_context(tc.tile_pool(name="ap3", bufs=4))
-        outp = ctx.enter_context(tc.tile_pool(name="outp", bufs=3))
+        ap3 = ctx.enter_context(tc.tile_pool(name="ap3", bufs=3))
+        outp = ctx.enter_context(tc.tile_pool(name="outp", bufs=2))
         pa = ctx.enter_context(tc.psum_pool(name="pa", bufs=2))
         pb = ctx.enter_context(tc.psum_pool(name="pb", bufs=2))
         pz = ctx.enter_context(tc.psum_pool(name="pz", bufs=2))
@@ -153,7 +153,7 @@ def tile_dynamicfeaturegroupinglayer_kernel(tc, x, W_masks, W1, W2, ln1_w, ln1_b
                 xs[g] = prepp.tile([P, M, B], U8, name="xs", tag="xs", align_bytes=64)
             nc.vector.quantize_mx(out=xc[g][:, m, :].bitcast(FP8X4), scales=xs[g][:, m, :], in_=wt[(g, m)][:])
 
-        sts, mvt, vet, rst, nbt = {}, {}, {}, {}, {}
+        sts, mvt, vet, nmt, rst, nbt = {}, {}, {}, {}, {}, {}
         ha, hb, zt, zbank, sig, r2, prod, finb = {}, {}, {}, {}, {}, {}, {}, {}
 
         def mx(t, second):
@@ -187,6 +187,8 @@ def tile_dynamicfeaturegroupinglayer_kernel(tc, x, W_masks, W1, W2, ln1_w, ln1_b
         def vn(t):
             vet[t] = small.tile([P, 2], F32, name="ve", tag="ve")
             nc.vector.tensor_scalar(out=vet[t][:], in0=mvt[t][:, :, 1], scalar1=EPS, scalar2=None, op0=ALU.add)
+            nmt[t] = small.tile([P, 2], F32, name="nm", tag="nm")
+            nc.vector.tensor_scalar(out=nmt[t][:], in0=mvt[t][:, :, 0], scalar1=-1.0, scalar2=None, op0=ALU.mult)
 
         def ch_rs(t):
             rst[t] = small.tile([P, 2], F32, name="rs", tag="rs")
@@ -194,8 +196,7 @@ def tile_dynamicfeaturegroupinglayer_kernel(tc, x, W_masks, W1, W2, ln1_w, ln1_b
 
         def ch_nb(t):
             nbt[t] = small.tile([P, 2], F32, name="nb", tag="nb")
-            nc.vector.scalar_tensor_tensor(out=nbt[t][:], in0=mvt[t][:, :, 0], scalar=-1.0, in1=rst[t][:],
-                                           op0=ALU.mult, op1=ALU.mult)
+            nc.gpsimd.tensor_tensor(out=nbt[t][:], in0=nmt[t][:], in1=rst[t][:], op=ALU.mult)
 
         def z_dst(t, w):
             ss, m = t // 4, t % 4
@@ -264,7 +265,6 @@ def tile_dynamicfeaturegroupinglayer_kernel(tc, x, W_masks, W1, W2, ln1_w, ln1_b
             else:
                 wfill_t(0, f, pb, "hb")
             wfill_copy(0, f, True)
-        nc.scalar.activation(out=warm[:], in_=one[:], func=ACT.Sigmoid)
         mps = pz.tile([P, 4, P], F32, name="mps", tag="zT")
         for u in range(2):
             for e in range(2):
@@ -326,17 +326,15 @@ def tile_dynamicfeaturegroupinglayer_kernel(tc, x, W_masks, W1, W2, ln1_w, ln1_b
                 mx(tb, True)
             if t < NSTEP:
                 bn(t)
-            if 0 <= tb < NSTEP:
-                ch_nb(tb)
             prep(t, prep_v1)
             if 0 <= t - 1 < NSTEP:
                 vn(t - 1)
                 ch_rs(t - 1)
+            prep(t, prep_v2)
             if 0 <= tb < NSTEP and t >= V_TAKES_Z:
                 z_vector(tb, 1)
             if t < NSTEP:
                 ag(t)
-            prep(t, prep_v2)
             if t + 1 < NSTEP:
                 mx(t + 1, False)
             if 0 <= ta < NSTEP:
@@ -344,6 +342,8 @@ def tile_dynamicfeaturegroupinglayer_kernel(tc, x, W_masks, W1, W2, ln1_w, ln1_b
                 tr(ta // 4, 2 * (ta % 4) + 1)
             if 0 <= tm < NSTEP:
                 mul(tm // 4, tm % 4, t - 1 >= V_TAKES_RELU)
+            if 0 <= t - 1 < NSTEP:
+                ch_nb(t - 1)
             if 0 <= tb < NSTEP:
                 z_scalar(tb, 0)
                 if t < V_TAKES_Z:

@@ -294,7 +294,7 @@ def tile_dynamicfeaturegroupinglayer_kernel(tc, x, W_masks, W1, W2, ln1_w, ln1_b
             if 0 <= k < 4:
                 weighted(g, k)
             elif 4 <= k < 8:
-                wfill_copy(g, k - 4, t < 8)
+                wfill_copy(g, k - 4, t < 8 or k == 7)
 
         def prep_v2(g, k, t):
             if k in (4, 5):

@@ -294,7 +294,7 @@ def tile_dynamicfeaturegroupinglayer_kernel(tc, x, W_masks, W1, W2, ln1_w, ln1_b
             if 0 <= k < 4:
                 weighted(g, k)
             elif 4 <= k < 8:
-                wfill_copy(g, k - 4, t < 8 or k == 7)
+                wfill_copy(g, k - 4, t < 8 or k == 6)
 
         def prep_v2(g, k, t):
             if k in (4, 5):

from contextlib import ExitStack

import concourse.mybir as mybir
from concourse.masks import make_identity

F32 = mybir.dt.float32
BF16 = mybir.dt.bfloat16
U32 = mybir.dt.uint32
U8 = mybir.dt.uint8
FP8X4 = mybir.dt.float8_e4m3fn_x4
ALU = mybir.AluOpType
ACT = mybir.ActivationFunctionType
AX = mybir.AxisListType

B, G, M, S, H = 256, 10, 4, 512, 512
ALPHA = 1.1
EPS = 1e-5
P = 128
FLOPS = 2 * 2 * B * G * M * S * H

NSTEP = G * 2 * M
NSS = G * 2
GM = G * M
V_TAKES_Z = 72
V_TAKES_RELU = 80


def tile_dynamicfeaturegroupinglayer_kernel(tc, x, W_masks, W1, W2, ln1_w, ln1_b, ln2_w, ln2_b, out):
    nc = tc.nc
    with ExitStack() as ctx:
        ctx.enter_context(tc.manual_schedule())
        const = ctx.enter_context(tc.tile_pool(name="const", bufs=1))
        wrawp = ctx.enter_context(tc.tile_pool(name="wrawp", bufs=3))
        prepp = ctx.enter_context(tc.tile_pool(name="prepp", bufs=2))
        wtp = ctx.enter_context(tc.tile_pool(name="wtp", bufs=4))
        small = ctx.enter_context(tc.tile_pool(name="small", bufs=4))
        zp = ctx.enter_context(tc.tile_pool(name="zp", bufs=2))
        ap3 = ctx.enter_context(tc.tile_pool(name="ap3", bufs=3))
        outp = ctx.enter_context(tc.tile_pool(name="outp", bufs=2))
        pa = ctx.enter_context(tc.psum_pool(name="pa", bufs=2))
        pb = ctx.enter_context(tc.psum_pool(name="pb", bufs=2))
        pz = ctx.enter_context(tc.psum_pool(name="pz", bufs=2))
        pprep = ctx.enter_context(tc.psum_pool(name="pprep", bufs=1))
        pfin = ctx.enter_context(tc.psum_pool(name="pfin", bufs=1))

        wm = const.tile([P, S], BF16, name="wm")
        nc.sync.dma_start(out=wm[0:GM, :], in_=W_masks.rearrange("g m s -> (g m) s"))
        x_sb = const.tile([P, 2, G * S], BF16, name="x_sb")
        for bh in range(2):
            nc.sync.dma_start(out=x_sb[:, bh, 0:S], in_=x[bh * P:(bh + 1) * P, 0:S])

        wraw = {}

        def load_w(g):
            t_ = wrawp.tile([P, 2, 4, S], BF16, name="wraw", tag="wraw")
            nc.sync.dma_start(out=t_[:, 0], in_=W1[g].rearrange("(t p) s -> p t s", p=P))
            nc.sync.dma_start(out=t_[:, 1], in_=W2[g].rearrange("(t p) s -> p t s", p=P))
            wraw[g] = t_

        load_w(0)
        lnraw = const.tile([P, 2, P], BF16, name="lnraw")
        nc.vector.memset(lnraw[:], 0.0)
        nc.sync.dma_start(out=lnraw[0:GM, 0, :], in_=ln1_w.rearrange("g (t p) -> (g t) p", p=P))
        nc.sync.dma_start(out=lnraw[GM:2 * GM, 0, :], in_=ln1_b.rearrange("g (t p) -> (g t) p", p=P))
        nc.sync.dma_start(out=lnraw[0:GM, 1, :], in_=ln2_w.rearrange("g (t p) -> (g t) p", p=P))
        nc.sync.dma_start(out=lnraw[GM:2 * GM, 1, :], in_=ln2_b.rearrange("g (t p) -> (g t) p", p=P))
        for bh in range(2):
            nc.sync.dma_start(out=x_sb[:, bh, S:G * S], in_=x[bh * P:(bh + 1) * P, S:G * S])
        load_w(1)

        ident = const.tile([P, P], F32, name="ident")
        make_identity(nc, ident[:])
        one = const.tile([P, 1], F32, name="one")
        nc.vector.memset(one[:], 1.0)
        warm = const.tile([P, 1], F32, name="warm")
        nc.scalar.activation(out=warm[:], in_=one[:], func=ACT.Exp)
        cexp = const.tile([P, 2], F32, name="cexp")
        nc.vector.memset(cexp[:], -0.5)
        cal = const.tile([P, 1], F32, name="cal")
        nc.vector.tensor_scalar(out=cal[:], in0=one[:], scalar1=-1.0 / ALPHA, scalar2=None, op0=ALU.mult)
        mask_sb = const.tile([P, S], F32, name="mask_sb")
        nc.vector.memset(mask_sb[:], 0.0)

        mx_ = const.tile([P, 1], F32, name="mx_")
        nc.vector.reduce_max(out=mx_[0:GM, :], in_=wm[0:GM, :], axis=AX.X)
        nmx = const.tile([P, 1], F32, name="nmx")
        nc.vector.tensor_scalar(out=nmx[0:GM, :], in0=mx_[0:GM, :], scalar1=-1.0, scalar2=None, op0=ALU.mult)
        nmxa = const.tile([P, 1], F32, name="nmxa")
        nc.vector.tensor_scalar(out=nmxa[0:GM, :], in0=mx_[0:GM, :], scalar1=-ALPHA, scalar2=None, op0=ALU.mult)
        ea_sb = const.tile([P, S], F32, name="ea_sb")
        sa = const.tile([P, 1], F32, name="sa")
        nc.scalar.activation(out=ea_sb[0:GM, :], in_=wm[0:GM, :], func=ACT.Exp, bias=nmxa[0:GM, :], scale=ALPHA,
                             accum_out=sa[0:GM, :])
        e_sb = const.tile([P, S], F32, name="e_sb")
        nc.scalar.activation(out=e_sb[0:GM, :], in_=wm[0:GM, :], func=ACT.Exp, bias=nmx[0:GM, :], scale=1.0)
        sae = const.tile([P, 1], F32, name="sae")
        nc.vector.tensor_scalar(out=sae[0:GM, :], in0=sa[0:GM, :], scalar1=EPS, scalar2=None, op0=ALU.add)
        msc = const.tile([P, 1], F32, name="msc")
        nc.gpsimd.tensor_tensor(out=msc[0:GM, :], in0=sae[0:GM, :], in1=cal[0:GM, :], op=ALU.pow)
        nc.vector.tensor_scalar(out=mask_sb[0:GM, :], in0=e_sb[0:GM, :], scalar1=msc[0:GM, :], scalar2=None,
                                op0=ALU.mult)
        lnf = const.tile([P, 2, P], F32, name="lnf")
        nc.vector.tensor_copy(out=lnf[:], in_=lnraw[:])

        gw, wc, ws, xc, xs, xbank, wt, fillb = {}, {}, {}, {}, {}, {}, {}, {}

        def wfill_t(g, f, pool, tag):
            w, jh = f // 2, f % 2
            bank = pool.tile([P, 2, 256], F32, name="wbank", tag=tag)
            for u in range(2):
                for jl in range(2):
                    src = wraw[g][:, w, 2 * jh + jl, :].bitcast(F32)
                    nc.tensor.transpose(bank[:, u, jl * P:(jl + 1) * P], src[:, P * u:P * (u + 1)], ident[:])
            fillb[(g, f)] = bank

        def wfill_copy(g, f, on_scalar):
            w, jh = f // 2, f % 2
            if jh == 0:
                gw[(g, w)] = prepp.tile([P, 4 * H], BF16, name="gw", tag="gw", align_bytes=64)
            dst = gw[(g, w)][:].bitcast(F32).rearrange("p (j u) -> p j u", u=2)
            src = fillb[(g, f)][:].rearrange("p u j -> p j u")
            if on_scalar:
                nc.scalar.copy(out=dst[:, jh * 256:(jh + 1) * 256, :], in_=src)
            else:
                nc.vector.tensor_copy(out=dst[:, jh * 256:(jh + 1) * 256, :], in_=src)

        def quant_w(g, w):
            if w == 0:
                wc[g] = prepp.tile([P, 2, H], U32, name="wc", tag="wc", align_bytes=64)
                ws[g] = prepp.tile([P, 2, H], U8, name="ws", tag="ws", align_bytes=64)
            nc.vector.quantize_mx(out=wc[g][:, w, :].bitcast(FP8X4), scales=ws[g][:, w, :], in_=gw[(g, w)][:])

        def x_t(g):
            bank = pprep.tile([P, 2, 256], F32, name="xbank", tag="prep")
            for u in range(2):
                for bh in range(2):
                    src = x_sb[:, bh, :].bitcast(F32)
                    nc.tensor.transpose(bank[:, u, bh * P:(bh + 1) * P],
                                        src[:, 256 * g + P * u:256 * g + P * (u + 1)], ident[:])
            xbank[g] = bank

        def weighted(g, m):
            t_ = wtp.tile([P, 4 * B], BF16, name="wt", tag="wt", align_bytes=64)
            in0 = xbank[g][:].rearrange("p u b -> p (u b)").bitcast(BF16).rearrange("p (u b e) -> p b u e", u=2, e=2)
            in1 = maskT[:, g * M + m, :].rearrange("p (u e) -> p u e", u=2).unsqueeze(1).to_broadcast([P, B, 2, 2])
            nc.vector.tensor_tensor(out=t_[:].rearrange("p (b u e) -> p b u e", u=2, e=2), in0=in0, in1=in1,
                                    op=ALU.mult)
            wt[(g, m)] = t_

        def quant_x(g, m):
            if m == 0:
                xc[g] = prepp.tile([P, M, B], U32, name="xc", tag="xc", align_bytes=64)
                xs[g] = prepp.tile([P, M, B], U8, name="xs", tag="xs", align_bytes=64)
            nc.vector.quantize_mx(out=xc[g][:, m, :].bitcast(FP8X4), scales=xs[g][:, m, :], in_=wt[(g, m)][:])

        sts, mvt, vet, nmt, rst, nbt = {}, {}, {}, {}, {}, {}
        ha, hb, zt, zbank, sig, r2, prod, finb = {}, {}, {}, {}, {}, {}, {}, {}

        def mx(t, second):
            g, bh, m = t // 8, (t % 8) // 4, t % 4
            cols = slice(bh * P, (bh + 1) * P)
            pair = []
            for w in range(2):
                if second:
                    bank = pb.tile([P, H], F32, name="hb", tag="hb")
                else:
                    bank = pa.tile([P, H], F32, name="ha", tag="ha")
                nc.tensor.matmul_mx(out=bank[:], lhsT=xc[g][:, m, cols].bitcast(FP8X4), lhsT_scale=xs[g][:, m, cols],
                                    rhs=wc[g][:, w, :].bitcast(FP8X4), rhs_scale=ws[g][:, w, :],
                                    start=True, stop=True)
                pair.append(bank)
            if second:
                hb[t] = pair
            else:
                ha[t] = pair

        def bn(t):
            sts[t] = small.tile([P, 2, 6], F32, name="st", tag="st")
            for w in range(2):
                nc.vector.bn_stats(out=sts[t][:, w, :], in_=ha[t][w][:])

        def ag(t):
            mvt[t] = small.tile([P, 2, 2], F32, name="mv", tag="mv")
            for w in range(2):
                nc.vector.bn_aggr(out=mvt[t][:, w, :], in_=sts[t][:, w, :])

        def vn(t):
            vet[t] = small.tile([P, 2], F32, name="ve", tag="ve")
            nc.vector.tensor_scalar(out=vet[t][:], in0=mvt[t][:, :, 1], scalar1=EPS, scalar2=None, op0=ALU.add)
            nmt[t] = small.tile([P, 2], F32, name="nm", tag="nm")
            nc.vector.tensor_scalar(out=nmt[t][:], in0=mvt[t][:, :, 0], scalar1=-1.0, scalar2=None, op0=ALU.mult)

        def ch_rs(t):
            rst[t] = small.tile([P, 2], F32, name="rs", tag="rs")
            nc.gpsimd.tensor_tensor(out=rst[t][:], in0=vet[t][:], in1=cexp[:], op=ALU.pow)

        def ch_nb(t):
            nbt[t] = small.tile([P, 2], F32, name="nb", tag="nb")
            nc.gpsimd.tensor_tensor(out=nbt[t][:], in0=nmt[t][:], in1=rst[t][:], op=ALU.mult)

        def z_dst(t, w):
            ss, m = t // 4, t % 4
            if ss not in zt:
                zt[ss] = zp.tile([P, 2, M, H], F32, name="z", tag="z")
            return zt[ss][:, w, m, :]

        def z_scalar(t, w):
            nc.scalar.activation(out=z_dst(t, w), in_=hb[t][w][:], func=ACT.Identity,
                                 bias=nbt[t][:, w:w + 1], scale=rst[t][:, w:w + 1])

        def z_vector(t, w):
            nc.vector.tensor_scalar(out=z_dst(t, w), in0=hb[t][w][:], scalar1=mvt[t][:, w, 0:1],
                                    scalar2=rst[t][:, w:w + 1], op0=ALU.subtract, op1=ALU.mult)

        def tr(ss, k):
            jt, w = k // 2, k % 2
            bank = pz.tile([P, M, P], F32, name="zT", tag="zT")
            for m in range(M):
                nc.tensor.transpose(bank[:, m, :], zt[ss][:, w, m, jt * P:(jt + 1) * P], ident[:])
            zbank[(ss, k)] = bank

        def act_sig(ss, jt):
            c = (ss // 2) * 4 + jt
            sig[(ss, jt)] = ap3.tile([P, M * P], F32, name="sig", tag="sig")
            nc.scalar.activation(out=sig[(ss, jt)][:], in_=zbank[(ss, 2 * jt)][:].rearrange("p m b -> p (m b)"),
                                 func=ACT.Sigmoid, bias=lnT[:, 0, GM + c:GM + c + 1], scale=lnT[:, 0, c:c + 1])

        def act_relu(ss, jt, on_vector):
            c = (ss // 2) * 4 + jt
            r2[(ss, jt)] = ap3.tile([P, M * P], F32, name="r2", tag="r2")
            src = zbank[(ss, 2 * jt + 1)][:].rearrange("p m b -> p (m b)")
            if on_vector:
                nc.vector.tensor_scalar(out=r2[(ss, jt)][:], in0=src, scalar1=lnT[:, 1, c:c + 1],
                                        scalar2=lnT[:, 1, GM + c:GM + c + 1], op0=ALU.mult, op1=ALU.add)
            else:
                nc.scalar.activation(out=r2[(ss, jt)][:], in_=src, func=ACT.Relu,
                                     bias=lnT[:, 1, GM + c:GM + c + 1], scale=lnT[:, 1, c:c + 1])

        def mul(ss, jt, on_vector):
            prod[(ss, jt)] = ap3.tile([P, M, P], F32, name="prod", tag="prod")
            dst = prod[(ss, jt)][:].rearrange("p m b -> p (m b)")
            if on_vector:
                nc.vector.scalar_tensor_tensor(out=dst, in0=r2[(ss, jt)][:], scalar=0.0, in1=sig[(ss, jt)][:],
                                               op0=ALU.max, op1=ALU.mult)
            else:
                nc.gpsimd.tensor_tensor(out=dst, in0=sig[(ss, jt)][:], in1=r2[(ss, jt)][:], op=ALU.mult)

        def acc(ss, jt):
            if jt == 0:
                finb[ss] = pfin.tile([P, H], F32, name="fin", tag="fin")
            for m in range(M):
                nc.tensor.matmul(finb[ss][:, jt * P:(jt + 1) * P], lhsT=prod[(ss, jt)][:, m, :], rhs=ident[:],
                                 is_transpose=True, start=(m == 0), stop=(m == M - 1))

        def fin(ss):
            g, bh = ss // 2, ss % 2
            ot = outp.tile([P, H], F32, name="ot", tag="ot")
            nc.scalar.copy(out=ot[:], in_=finb[ss][:])
            nc.sync.dma_start(out=out[bh * P:(bh + 1) * P, g * H:(g + 1) * H], in_=ot[:])

        x_t(0)
        for f in range(4):
            if f < 2:
                wfill_t(0, f, pa, "ha")
            else:
                wfill_t(0, f, pb, "hb")
            wfill_copy(0, f, True)
        mps = pz.tile([P, 4, P], F32, name="mps", tag="zT")
        for u in range(2):
            for e in range(2):
                nc.tensor.transpose(mps[:, 2 * u + e, :], mask_sb[:, 256 * u + e:256 * (u + 1):2], ident[:])
        lps = pz.tile([P, 2, P], F32, name="lps", tag="zT")
        for a in range(2):
            nc.tensor.transpose(lps[:, a, :], lnf[:, a, :], ident[:])
        quant_w(0, 0)
        maskT = const.tile([P, GM, 4], F32, name="maskT")
        nc.vector.tensor_copy(out=maskT[:], in_=mps[:, :, 0:GM].rearrange("p t c -> p c t"))
        weighted(0, 0)
        quant_w(0, 1)
        quant_x(0, 0)
        mx(0, False)
        weighted(0, 1)
        lnT = const.tile([P, 2, P], F32, name="lnT")
        nc.vector.tensor_copy(out=lnT[:], in_=lps[:])
        quant_x(0, 1)
        weighted(0, 2)
        weighted(0, 3)
        quant_x(0, 2)
        x_t(1)
        quant_x(0, 3)
        weighted(1, 0)

        def prep_v1(g, k, t):
            if 0 <= k < 4:
                weighted(g, k)
            elif 4 <= k < 8:
                wfill_copy(g, k - 4, t < 8 or k == 6)

        def prep_v2(g, k, t):
            if k in (4, 5):
                quant_x(g, 2 * k - 8)
                quant_x(g, 2 * k - 7)
            elif k in (6, 7):
                quant_w(g, k - 6)

        def prep_pe(g, k, t):
            if k == -1:
                x_t(g)
            elif 3 <= k < 7:
                wfill_t(g, k - 3, pprep, "prep")

        def prep(t, part):
            for gq in range(1, G):
                k = t - (8 * (gq - 1) - 1)
                if -1 <= k <= 7:
                    part(gq, k, t)

        for t in range(NSTEP + 8):
            tb = t - 2
            ta = tb - 4
            tm = ta - 1
            tf = tm - 1
            if t % 8 == 0 and t // 8 + 2 < G:
                load_w(t // 8 + 2)
            if 0 <= tb < NSTEP:
                mx(tb, True)
            if t < NSTEP:
                bn(t)
            prep(t, prep_v1)
            if 0 <= t - 1 < NSTEP:
                vn(t - 1)
                ch_rs(t - 1)
            prep(t, prep_v2)
            if 0 <= tb < NSTEP and t >= V_TAKES_Z:
                z_vector(tb, 1)
            if t < NSTEP:
                ag(t)
            if t + 1 < NSTEP:
                mx(t + 1, False)
            if 0 <= ta < NSTEP:
                tr(ta // 4, 2 * (ta % 4))
                tr(ta // 4, 2 * (ta % 4) + 1)
            if 0 <= tm < NSTEP:
                mul(tm // 4, tm % 4, t - 1 >= V_TAKES_RELU)
            if 0 <= t - 1 < NSTEP:
                ch_nb(t - 1)
            if 0 <= tb < NSTEP:
                z_scalar(tb, 0)
                if t < V_TAKES_Z:
                    z_scalar(tb, 1)
            if 0 <= ta < NSTEP:
                act_sig(ta // 4, ta % 4)
                act_relu(ta // 4, ta % 4, t >= V_TAKES_RELU)
            if 0 <= tf < NSTEP:
                acc(tf // 4, tf % 4)
                if tf % 4 == 3:
                    fin(tf // 4)
            prep(t, prep_pe)
